import numpy as np
import ml_dtypes


def mxq(x, axis, fmt="e4m3"):
    dtype, down = {"e4m3": (ml_dtypes.float8_e4m3fn, 7), "e5m2": (ml_dtypes.float8_e5m2, 14)}[fmt]
    v = np.moveaxis(np.asarray(x, np.float32).astype(ml_dtypes.bfloat16).astype(np.float64), axis, -1)
    blocks = v.reshape(v.shape[:-1] + (-1, 32))
    amax = np.abs(blocks).max(-1, keepdims=True)
    byte = np.maximum(np.where(amax > 0, np.frexp(amax)[1] - 1 + 127, 0) - down, 1)
    scale = np.exp2(byte - 127.0)
    codes = (blocks / scale).astype(np.float32).astype(dtype).astype(np.float64)
    return np.moveaxis((codes * scale).reshape(v.shape), -1, axis)


WIDE = False


def mx_kscale(k):
    if not WIDE:
        return np.ones(k)
    levels = np.array([10, -10, 5, -5, 0])
    if k % 512:
        return np.exp2(np.random.permutation(np.resize(levels, k // 32))).repeat(32)
    a = np.empty((k // 512, 16))
    for p in range(k // 512):
        a[p, :8] = np.random.permutation(np.resize(levels, 8))
        for g in range(8):
            far = levels[np.abs(levels - a[p, g]) >= 10]
            a[p, g + 8] = far[np.random.randint(len(far))]
    return np.exp2(a.ravel()).repeat(32)


BF16 = ml_dtypes.bfloat16


def bf(x):
    return np.asarray(x, np.float32).astype(BF16)


def f64(x):
    return np.asarray(x).astype(np.float64)


B, N, DIM, H, KD, D = 32, 256, 512, 4, 16, 32
HD = 2 * KD + D
HQKV = H * HD
EPS = 1e-5


def setup_inputs():
    s = mx_kscale(DIM)
    c = 2.0 ** (-8.0 * np.random.random(HQKV))
    x = np.random.standard_normal((B, N, DIM)) + 0.5 * np.random.standard_normal(DIM)
    return {"x": bf(x * s),
            "qkv_w": bf(np.random.standard_normal((HQKV, DIM)) * c[:, None] / np.sqrt(DIM) / s),
            "qkv_g": bf(2.0 + 0.2 * np.random.standard_normal(HQKV)),
            "qkv_b": bf(0.3 * np.random.standard_normal(HQKV))}


def bn(y, g, b):
    m = y.mean(axis=(0, 1))
    v = ((y - m) ** 2).mean(axis=(0, 1))
    return (y - m) * (g / np.sqrt(v + EPS)) + b


def reference(x, qkv_w, qkv_g, qkv_b):
    y = mxq(f64(x), 2, "e4m3") @ mxq(f64(qkv_w), 1, "e4m3").T
    qkv = bn(y, f64(qkv_g), f64(qkv_b)).reshape(B, N, H, HD)
    q = qkv[..., :KD].transpose(0, 2, 1, 3)
    k = qkv[..., KD:2 * KD].transpose(0, 2, 1, 3)
    v = qkv[..., 2 * KD:].transpose(0, 2, 1, 3)
    return q, k, v

@@ -1,0 +1,264 @@
+from contextlib import ExitStack
+
+import concourse.mybir as mybir
+from concourse.masks import make_identity
+
+F32 = mybir.dt.float32
+BF16 = mybir.dt.bfloat16
+U32 = mybir.dt.uint32
+U8 = mybir.dt.uint8
+FP8X4 = mybir.dt.float8_e4m3fn_x4
+ACT = mybir.ActivationFunctionType
+ALU = mybir.AluOpType
+
+P = 128
+BATCHES, TOKENS, CHANNELS = 32, 256, 512
+HEADS, QK_DIM, V_DIM = 4, 16, 32
+HEAD_FEATURES = 2 * QK_DIM + V_DIM
+FEATURES = HEADS * HEAD_FEATURES
+HALVES = FEATURES // P
+ROWS = BATCHES * TOKENS
+EPS = 1e-5
+
+PACK = 4
+WORDS = CHANNELS // 2
+WORD_PLANES = WORDS // P
+
+BANK = 512
+UNIT_TOKENS = BANK // P
+GROUP_TOKENS = 8
+GROUP_UNITS = GROUP_TOKENS // UNIT_TOKENS
+GROUP_BATCHES = P * GROUP_TOKENS // TOKENS
+RUNS = TOKENS // GROUP_TOKENS
+UNITS = ROWS // BANK
+BN_STATS_DIM = 6
+LAG = 2
+
+PARTS = (
+    (0, QK_DIM, 0),
+    (QK_DIM, QK_DIM, HEADS * QK_DIM),
+    (2 * QK_DIM, V_DIM, 2 * HEADS * QK_DIM),
+)
+
+FLOPS = 2 * ROWS * CHANNELS * FEATURES
+
+
+def tile_attention_pa_t_kernel(tc, x, qkv_w, qkv_g, qkv_b, out_q, out_k, out_v):
+    nc = tc.nc
+    with ExitStack() as ctx:
+        const = ctx.enter_context(tc.tile_pool(name="const", bufs=1))
+        x_pool = ctx.enter_context(tc.tile_pool(name="x_rows", bufs=UNITS))
+        grouped_pool = ctx.enter_context(tc.tile_pool(name="grouped", bufs=3))
+        zt_pool = ctx.enter_context(tc.tile_pool(name="zt", bufs=HALVES * (LAG + 1)))
+        stage_pool = ctx.enter_context(tc.tile_pool(name="stage", bufs=3))
+        psum_t = ctx.enter_context(tc.psum_pool(name="psum_t", bufs=4))
+        psum_y = ctx.enter_context(tc.psum_pool(name="psum_y", bufs=4))
+        ctx.enter_context(tc.manual_schedule())
+
+        gb_rows = const.tile([P, FEATURES], BF16)
+        nc.vector.memset(gb_rows[:], 0.0)
+        nc.scalar.dma_start(out=gb_rows[0:1, :], in_=qkv_g.rearrange("(o f) -> o f", o=1))
+        nc.scalar.dma_start(out=gb_rows[1:2, :], in_=qkv_b.rearrange("(o f) -> o f", o=1))
+        w_rows = const.tile([P, HALVES * CHANNELS], BF16)
+        nc.sync.dma_start(
+            out=w_rows[:].rearrange("p (s k) -> p s k", s=HALVES),
+            in_=qkv_w.rearrange("(s p) k -> p s k", s=HALVES),
+        )
+        x_units = x.flatten_outer_dims().rearrange(
+            "(g p s t) k -> g s p (t k)", p=P, s=GROUP_UNITS, t=UNIT_TOKENS
+        )
+        x_rows = []
+        for unit in range(UNITS):
+            x_tile = x_pool.tile([P, UNIT_TOKENS * CHANNELS], BF16, name="x_tile")
+            nc.sync.dma_start(out=x_tile[:], in_=x_units[unit // GROUP_UNITS, unit % GROUP_UNITS])
+            x_rows.append(x_tile)
+
+        one = const.tile([P, 1], F32)
+        nc.vector.memset(one[:], 1.0)
+        table_warm = const.tile([P, 1], F32)
+        nc.scalar.activation(out=table_warm[:], in_=one[:], func=ACT.Sqrt)
+
+        identity = const.tile([P, P], F32)
+        make_identity(nc, identity[:])
+        row_order = const.tile([P, P], F32)
+        nc.vector.tensor_copy(
+            out=row_order[:].rearrange("p (r b) -> p r b", b=GROUP_BATCHES),
+            in_=identity[:].rearrange("p (b r) -> p r b", b=GROUP_BATCHES),
+        )
+
+        gb_sorted = const.tile([P, FEATURES], F32)
+        gb_by_head = gb_rows[:].rearrange("p (h j) -> p h j", h=HEADS)
+        for first, width, base in PARTS:
+            nc.vector.tensor_copy(
+                out=gb_sorted[:, base : base + HEADS * width].rearrange("p (h j) -> p h j", h=HEADS),
+                in_=gb_by_head[:, :, first : first + width],
+            )
+
+        w_words = w_rows[:].bitcast(F32)
+        wt = psum_t.tile([P, HALVES, WORD_PLANES, P], F32, tag="t")
+        for s in range(HALVES):
+            for u in range(WORD_PLANES):
+                words_u = slice(s * WORDS + u, (s + 1) * WORDS, WORD_PLANES)
+                nc.tensor.transpose(wt[:, s, u, :], w_words[:, words_u], identity[:])
+        w_grouped = const.tile([P, FEATURES * PACK], BF16, align_bytes=64)
+        w_grouped_words = w_grouped[:].bitcast(F32).rearrange("p (f u) -> p f u", u=WORD_PLANES)
+        heads_here = HEADS // HALVES
+        for s in range(HALVES):
+            by_head = wt[:, s].rearrange("p u (h j) -> p h j u", h=heads_here)
+            for first, width, base in PARTS:
+                start = base + s * heads_here * width
+                nc.vector.tensor_copy(
+                    out=w_grouped_words[:, start : start + heads_here * width, :].rearrange(
+                        "p (h j) u -> p h j u", h=heads_here
+                    ),
+                    in_=by_head[:, :, first : first + width, :],
+                )
+        w_codes = const.tile([P, FEATURES], U32, align_bytes=64)
+        w_scales = const.tile([P, FEATURES], U8, align_bytes=64)
+        nc.vector.quantize_mx(out=w_codes[:].bitcast(FP8X4), scales=w_scales[:], in_=w_grouped[:])
+
+        gb_t = psum_t.tile([P, HALVES, P], F32, tag="t")
+        for half in range(HALVES):
+            nc.tensor.transpose(gb_t[:, half, :], gb_sorted[:, half * P : (half + 1) * P], identity[:])
+        gain_shift = const.tile([P, HALVES, 2], F32)
+        nc.vector.tensor_copy(out=gain_shift[:], in_=gb_t[:, :, 0:2])
+
+        x_codes = const.tile([P, ROWS], U32, align_bytes=64)
+        x_scales = const.tile([P, ROWS], U8, align_bytes=64)
+
+        def multiply(unit):
+            cols = slice(unit * BANK, (unit + 1) * BANK)
+            banks = []
+            for half in range(HALVES):
+                features = slice(half * P, (half + 1) * P)
+                y = psum_y.tile([P, BANK], F32, tag="y")
+                nc.tensor.matmul_mx(
+                    out=y[:],
+                    lhsT=w_codes[:, features].bitcast(FP8X4),
+                    lhsT_scale=w_scales[:, features],
+                    rhs=x_codes[:, cols].bitcast(FP8X4),
+                    rhs_scale=x_scales[:, cols],
+                    start=True,
+                    stop=True,
+                )
+                banks.append(y)
+            return banks
+
+        stats = const.tile([P, HALVES, UNITS, BN_STATS_DIM], F32)
+        grouped_of = {}
+
+        def transpose_x(unit):
+            words = x_rows[unit][:].bitcast(F32)
+            grouped = grouped_pool.tile([P, BANK * PACK], BF16, align_bytes=64)
+            grouped_words = grouped[:].bitcast(F32).rearrange(
+                "p (t c u) -> p t c u", t=UNIT_TOKENS, u=WORD_PLANES
+            )
+            tokens_per_bank = BANK // WORDS
+            for first_token in range(0, UNIT_TOKENS, tokens_per_bank):
+                xt = psum_t.tile([P, tokens_per_bank, WORD_PLANES, P], F32, tag="t")
+                for t in range(tokens_per_bank):
+                    for u in range(WORD_PLANES):
+                        token = first_token + t
+                        words_u = slice(token * WORDS + u, (token + 1) * WORDS, WORD_PLANES)
+                        nc.tensor.transpose(xt[:, t, u, :], words[:, words_u], row_order[:])
+                nc.scalar.copy(
+                    out=grouped_words[:, first_token : first_token + tokens_per_bank],
+                    in_=xt[:].rearrange("p t u c -> p t c u"),
+                )
+            grouped_of[unit] = grouped
+
+        def quantise_x(unit):
+            cols = slice(unit * BANK, (unit + 1) * BANK)
+            nc.vector.quantize_mx(
+                out=x_codes[:, cols].bitcast(FP8X4),
+                scales=x_scales[:, cols],
+                in_=grouped_of[unit][:],
+            )
+
+        def measure(unit):
+            for half, y in enumerate(multiply(unit)):
+                nc.vector.bn_stats(out=stats[:, half, unit, :], in_=y[:])
+
+        for step in range(UNITS + LAG):
+            if step < UNITS:
+                transpose_x(step)
+            if 1 <= step <= UNITS:
+                quantise_x(step - 1)
+            if step >= LAG:
+                measure(step - LAG)
+
+        mean_var = const.tile([P, HALVES, 2], F32)
+        for half in range(HALVES):
+            nc.vector.bn_aggr(
+                out=mean_var[:, half, :], in_=stats[:, half].rearrange("p u s -> p (u s)")
+            )
+        var_eps = const.tile([P, HALVES], F32)
+        nc.vector.tensor_scalar(
+            out=var_eps[:], in0=mean_var[:, :, 1], scalar1=EPS, scalar2=None, op0=ALU.add
+        )
+        std = const.tile([P, HALVES], F32)
+        nc.scalar.activation(out=std[:], in_=var_eps[:], func=ACT.Sqrt)
+        inv_std = const.tile([P, HALVES], F32)
+        nc.vector.reciprocal(out=inv_std[:], in_=std[:])
+        scale = const.tile([P, HALVES], F32)
+        nc.vector.tensor_tensor(out=scale[:], in0=gain_shift[:, :, 0], in1=inv_std[:], op=ALU.mult)
+        mean_scaled = const.tile([P, HALVES], F32)
+        nc.vector.tensor_tensor(out=mean_scaled[:], in0=mean_var[:, :, 0], in1=scale[:], op=ALU.mult)
+        shift = const.tile([P, HALVES], F32)
+        nc.vector.tensor_tensor(
+            out=shift[:], in0=gain_shift[:, :, 1], in1=mean_scaled[:], op=ALU.subtract
+        )
+
+        zt_of = {}
+        stage_of = {}
+
+        def normalise(unit):
+            tiles = []
+            for half, y in enumerate(multiply(unit)):
+                zt = zt_pool.tile([P, BANK], F32)
+                nc.scalar.activation(
+                    out=zt[:],
+                    in_=y[:],
+                    func=ACT.Identity,
+                    bias=shift[:, half : half + 1],
+                    scale=scale[:, half : half + 1],
+                )
+                tiles.append(zt)
+            zt_of[unit] = tiles
+
+        def collect(unit):
+            group, part = divmod(unit, GROUP_UNITS)
+            if part == 0:
+                stage_qk = stage_pool.tile([P, 2 * HEADS, GROUP_TOKENS, QK_DIM], F32)
+                stage_v = stage_pool.tile([P, HEADS, GROUP_TOKENS, V_DIM], F32)
+                stage_of[group] = (stage_qk, stage_v)
+            tokens = slice(part * UNIT_TOKENS, (part + 1) * UNIT_TOKENS)
+            for zt, stage, width in zip(zt_of[unit], stage_of[group], (QK_DIM, V_DIM)):
+                z = psum_t.tile([P, UNIT_TOKENS, P], F32, tag="t")
+                for t in range(UNIT_TOKENS):
+                    nc.tensor.transpose(z[:, t, :], zt[:, t * P : (t + 1) * P], identity[:])
+                nc.vector.tensor_copy(
+                    out=stage[:, :, tokens, :], in_=z[:].rearrange("p t (a j) -> p a t j", j=width)
+                )
+
+        def store(group):
+            stage_qk, stage_v = stage_of[group]
+            for b in range(GROUP_BATCHES):
+                batch = group * GROUP_BATCHES + b
+                for out, rows in (
+                    (out_q, stage_qk[b:P:GROUP_BATCHES, 0:HEADS]),
+                    (out_k, stage_qk[b:P:GROUP_BATCHES, HEADS : 2 * HEADS]),
+                    (out_v, stage_v[b:P:GROUP_BATCHES]),
+                ):
+                    nc.sync.dma_start(
+                        out=out[batch].rearrange("h (r t) j -> r h (t j)", t=GROUP_TOKENS),
+                        in_=rows.rearrange("p h t j -> p h (t j)"),
+                    )
+
+        for step in range(UNITS + LAG):
+            if step < UNITS:
+                normalise(step)
+            if step >= LAG:
+                collect(step - LAG)
+                if (step - LAG) % GROUP_UNITS == GROUP_UNITS - 1:
+                    store((step - LAG) // GROUP_UNITS)

@@ -49,16 +49,14 @@ def tile_attention_pa_t_kernel(tc, x, qkv_w, qkv_g, qkv_b, out_q, out_k, out_v):
         const = ctx.enter_context(tc.tile_pool(name="const", bufs=1))
         x_pool = ctx.enter_context(tc.tile_pool(name="x_rows", bufs=UNITS))
         grouped_pool = ctx.enter_context(tc.tile_pool(name="grouped", bufs=3))
-        zt_pool = ctx.enter_context(tc.tile_pool(name="zt", bufs=HALVES * (LAG + 1)))
+        zt_pool = ctx.enter_context(tc.tile_pool(name="zt", bufs=3))
+        scaled_pool = ctx.enter_context(tc.tile_pool(name="scaled", bufs=3))
         stage_pool = ctx.enter_context(tc.tile_pool(name="stage", bufs=3))
-        psum_t = ctx.enter_context(tc.psum_pool(name="psum_t", bufs=4))
-        psum_y = ctx.enter_context(tc.psum_pool(name="psum_y", bufs=4))
+        psum = ctx.enter_context(tc.psum_pool(name="psum", bufs=8))
         ctx.enter_context(tc.manual_schedule())
 
         gb_rows = const.tile([P, FEATURES], BF16)
-        nc.vector.memset(gb_rows[:], 0.0)
-        nc.scalar.dma_start(out=gb_rows[0:1, :], in_=qkv_g.rearrange("(o f) -> o f", o=1))
-        nc.scalar.dma_start(out=gb_rows[1:2, :], in_=qkv_b.rearrange("(o f) -> o f", o=1))
+        nc.gpsimd.memset(gb_rows[:], 0.0)
         w_rows = const.tile([P, HALVES * CHANNELS], BF16)
         nc.sync.dma_start(
             out=w_rows[:].rearrange("p (s k) -> p s k", s=HALVES),
@@ -70,8 +68,16 @@ def tile_attention_pa_t_kernel(tc, x, qkv_w, qkv_g, qkv_b, out_q, out_k, out_v):
         x_rows = []
         for unit in range(UNITS):
             x_tile = x_pool.tile([P, UNIT_TOKENS * CHANNELS], BF16, name="x_tile")
-            nc.sync.dma_start(out=x_tile[:], in_=x_units[unit // GROUP_UNITS, unit % GROUP_UNITS])
+            source = x_units[unit // GROUP_UNITS, unit % GROUP_UNITS]
+            pieces = 2 if unit == 0 else 1
+            width = UNIT_TOKENS * CHANNELS // pieces
+            for piece in range(pieces):
+                cols = slice(piece * width, (piece + 1) * width)
+                nc.sync.dma_start(out=x_tile[:, cols], in_=source[:, cols])
             x_rows.append(x_tile)
+            if unit == 3:
+                nc.sync.dma_start(out=gb_rows[0:1, :], in_=qkv_g.rearrange("(o f) -> o f", o=1))
+                nc.sync.dma_start(out=gb_rows[1:2, :], in_=qkv_b.rearrange("(o f) -> o f", o=1))
 
         one = const.tile([P, 1], F32)
         nc.vector.memset(one[:], 1.0)
@@ -86,16 +92,8 @@ def tile_attention_pa_t_kernel(tc, x, qkv_w, qkv_g, qkv_b, out_q, out_k, out_v):
             in_=identity[:].rearrange("p (b r) -> p r b", b=GROUP_BATCHES),
         )
 
-        gb_sorted = const.tile([P, FEATURES], F32)
-        gb_by_head = gb_rows[:].rearrange("p (h j) -> p h j", h=HEADS)
-        for first, width, base in PARTS:
-            nc.vector.tensor_copy(
-                out=gb_sorted[:, base : base + HEADS * width].rearrange("p (h j) -> p h j", h=HEADS),
-                in_=gb_by_head[:, :, first : first + width],
-            )
-
         w_words = w_rows[:].bitcast(F32)
-        wt = psum_t.tile([P, HALVES, WORD_PLANES, P], F32, tag="t")
+        wt = psum.tile([P, HALVES, WORD_PLANES, P], F32, tag="bank")
         for s in range(HALVES):
             for u in range(WORD_PLANES):
                 words_u = slice(s * WORDS + u, (s + 1) * WORDS, WORD_PLANES)
@@ -117,32 +115,60 @@ def tile_attention_pa_t_kernel(tc, x, qkv_w, qkv_g, qkv_b, out_q, out_k, out_v):
         w_scales = const.tile([P, FEATURES], U8, align_bytes=64)
         nc.vector.quantize_mx(out=w_codes[:].bitcast(FP8X4), scales=w_scales[:], in_=w_grouped[:])
 
-        gb_t = psum_t.tile([P, HALVES, P], F32, tag="t")
-        for half in range(HALVES):
-            nc.tensor.transpose(gb_t[:, half, :], gb_sorted[:, half * P : (half + 1) * P], identity[:])
+        gb_sorted = const.tile([P, FEATURES], F32)
         gain_shift = const.tile([P, HALVES, 2], F32)
-        nc.vector.tensor_copy(out=gain_shift[:], in_=gb_t[:, :, 0:2])
+
+        def sort_gain_shift():
+            gb_by_head = gb_rows[:].rearrange("p (h j) -> p h j", h=HEADS)
+            for first, width, base in PARTS:
+                nc.vector.tensor_copy(
+                    out=gb_sorted[:, base : base + HEADS * width].rearrange(
+                        "p (h j) -> p h j", h=HEADS
+                    ),
+                    in_=gb_by_head[:, :, first : first + width],
+                )
+
+        def turn_gain_shift():
+            gb_t = psum.tile([P, HALVES, P], F32, tag="bank")
+            for half in range(HALVES):
+                nc.tensor.transpose(
+                    gb_t[:, half, :], gb_sorted[:, half * P : (half + 1) * P], identity[:]
+                )
+            nc.vector.tensor_copy(out=gain_shift[:], in_=gb_t[:, :, 0:2])
 
         x_codes = const.tile([P, ROWS], U32, align_bytes=64)
         x_scales = const.tile([P, ROWS], U8, align_bytes=64)
 
-        def multiply(unit):
+        def multiply(unit, half):
             cols = slice(unit * BANK, (unit + 1) * BANK)
-            banks = []
-            for half in range(HALVES):
-                features = slice(half * P, (half + 1) * P)
-                y = psum_y.tile([P, BANK], F32, tag="y")
+            features = slice(half * P, (half + 1) * P)
+            y = psum.tile([P, BANK], F32, tag="bank")
+            nc.tensor.matmul_mx(
+                out=y[:],
+                lhsT=w_codes[:, features].bitcast(FP8X4),
+                lhsT_scale=w_scales[:, features],
+                rhs=x_codes[:, cols].bitcast(FP8X4),
+                rhs_scale=x_scales[:, cols],
+                start=True,
+                stop=True,
+            )
+            return y
+
+        def multiply_rows(unit, half):
+            features = slice(half * P, (half + 1) * P)
+            y = psum.tile([P, UNIT_TOKENS, P], F32, tag="bank")
+            for t in range(UNIT_TOKENS):
+                rows = slice(unit * BANK + t * P, unit * BANK + (t + 1) * P)
                 nc.tensor.matmul_mx(
-                    out=y[:],
-                    lhsT=w_codes[:, features].bitcast(FP8X4),
-                    lhsT_scale=w_scales[:, features],
-                    rhs=x_codes[:, cols].bitcast(FP8X4),
-                    rhs_scale=x_scales[:, cols],
+                    out=y[:, t, :],
+                    lhsT=x_codes[:, rows].bitcast(FP8X4),
+                    lhsT_scale=x_scales[:, rows],
+                    rhs=w_codes[:, features].bitcast(FP8X4),
+                    rhs_scale=w_scales[:, features],
                     start=True,
                     stop=True,
                 )
-                banks.append(y)
-            return banks
+            return y
 
         stats = const.tile([P, HALVES, UNITS, BN_STATS_DIM], F32)
         grouped_of = {}
@@ -155,7 +181,7 @@ def tile_attention_pa_t_kernel(tc, x, qkv_w, qkv_g, qkv_b, out_q, out_k, out_v):
             )
             tokens_per_bank = BANK // WORDS
             for first_token in range(0, UNIT_TOKENS, tokens_per_bank):
-                xt = psum_t.tile([P, tokens_per_bank, WORD_PLANES, P], F32, tag="t")
+                xt = psum.tile([P, tokens_per_bank, WORD_PLANES, P], F32, tag="bank")
                 for t in range(tokens_per_bank):
                     for u in range(WORD_PLANES):
                         token = first_token + t
@@ -175,8 +201,11 @@ def tile_attention_pa_t_kernel(tc, x, qkv_w, qkv_g, qkv_b, out_q, out_k, out_v):
                 in_=grouped_of[unit][:],
             )
 
+        banks_of = {}
+
         def measure(unit):
-            for half, y in enumerate(multiply(unit)):
+            banks_of[unit] = [multiply(unit, half) for half in range(HALVES)]
+            for half, y in enumerate(banks_of[unit]):
                 nc.vector.bn_stats(out=stats[:, half, unit, :], in_=y[:])
 
         for step in range(UNITS + LAG):
@@ -186,6 +215,18 @@ def tile_attention_pa_t_kernel(tc, x, qkv_w, qkv_g, qkv_b, out_q, out_k, out_v):
                 quantise_x(step - 1)
             if step >= LAG:
                 measure(step - LAG)
+            if step == UNITS // 2:
+                sort_gain_shift()
+            if step == UNITS // 2 + 1:
+                turn_gain_shift()
+
+        order = list(range(UNITS - LAG, UNITS)) + list(range(UNITS - LAG))
+        y_qk = {unit: banks_of[unit][0] for unit in order[:LAG]}
+        y_v = {}
+        affine_bank = psum.tile([P, 2, P], F32, tag="bank")
+        for unit in order[:LAG]:
+            y_v[unit] = multiply_rows(unit, 1)
+        y_qk[order[LAG]] = multiply(order[LAG], 0)
 
         mean_var = const.tile([P, HALVES, 2], F32)
         for half in range(HALVES):
@@ -209,37 +250,70 @@ def tile_attention_pa_t_kernel(tc, x, qkv_w, qkv_g, qkv_b, out_q, out_k, out_v):
             out=shift[:], in0=gain_shift[:, :, 1], in1=mean_scaled[:], op=ALU.subtract
         )
 
+        for i, column in enumerate((scale, shift)):
+            nc.tensor.matmul(
+                affine_bank[:, i, :],
+                lhsT=column[:, 1:2].to_broadcast([P, P]),
+                rhs=identity[:],
+                start=True,
+                stop=True,
+            )
+        affine_rows = const.tile([P, 2, P], F32)
+        nc.vector.tensor_copy(out=affine_rows[:], in_=affine_bank[:])
+        y_v[order[LAG]] = multiply_rows(order[LAG], 1)
+
         zt_of = {}
+        scaled_of = {}
         stage_of = {}
 
-        def normalise(unit):
-            tiles = []
-            for half, y in enumerate(multiply(unit)):
-                zt = zt_pool.tile([P, BANK], F32)
-                nc.scalar.activation(
-                    out=zt[:],
-                    in_=y[:],
-                    func=ACT.Identity,
-                    bias=shift[:, half : half + 1],
-                    scale=scale[:, half : half + 1],
-                )
-                tiles.append(zt)
-            zt_of[unit] = tiles
+        def normalise_qk(unit):
+            zt = zt_pool.tile([P, BANK], F32)
+            nc.scalar.activation(
+                out=zt[:], in_=y_qk[unit][:], func=ACT.Identity, bias=shift[:, 0:1], scale=scale[:, 0:1]
+            )
+            zt_of[unit] = zt
 
-        def collect(unit):
-            group, part = divmod(unit, GROUP_UNITS)
-            if part == 0:
-                stage_qk = stage_pool.tile([P, 2 * HEADS, GROUP_TOKENS, QK_DIM], F32)
-                stage_v = stage_pool.tile([P, HEADS, GROUP_TOKENS, V_DIM], F32)
-                stage_of[group] = (stage_qk, stage_v)
-            tokens = slice(part * UNIT_TOKENS, (part + 1) * UNIT_TOKENS)
-            for zt, stage, width in zip(zt_of[unit], stage_of[group], (QK_DIM, V_DIM)):
-                z = psum_t.tile([P, UNIT_TOKENS, P], F32, tag="t")
-                for t in range(UNIT_TOKENS):
-                    nc.tensor.transpose(z[:, t, :], zt[:, t * P : (t + 1) * P], identity[:])
-                nc.vector.tensor_copy(
-                    out=stage[:, :, tokens, :], in_=z[:].rearrange("p t (a j) -> p a t j", j=width)
-                )
+        def scale_v(unit):
+            scaled = scaled_pool.tile([P, UNIT_TOKENS, P], F32)
+            nc.vector.tensor_tensor(
+                out=scaled[:],
+                in0=y_v[unit][:],
+                in1=affine_rows[:, 0:1, :].to_broadcast([P, UNIT_TOKENS, P]),
+                op=ALU.mult,
+            )
+            scaled_of[unit] = scaled
+
+        def open_stages(group):
+            stage_qk = stage_pool.tile([P, 2 * HEADS, GROUP_TOKENS, QK_DIM], F32)
+            stage_v = stage_pool.tile([P, HEADS, GROUP_TOKENS, V_DIM], F32)
+            stage_of[group] = (stage_qk, stage_v)
+
+        def unit_tokens(unit):
+            part = unit % GROUP_UNITS
+            return slice(part * UNIT_TOKENS, (part + 1) * UNIT_TOKENS)
+
+        def collect_qk(unit):
+            tokens = unit_tokens(unit)
+            stage_qk = stage_of[unit // GROUP_UNITS][0]
+            z = psum.tile([P, UNIT_TOKENS, P], F32, tag="bank")
+            for t in range(UNIT_TOKENS):
+                nc.tensor.transpose(z[:, t, :], zt_of[unit][:, t * P : (t + 1) * P], identity[:])
+            nc.scalar.copy(
+                out=stage_qk[:, :, tokens, :], in_=z[:].rearrange("p t (a j) -> p a t j", j=QK_DIM)
+            )
+
+        def shift_v(unit):
+            tokens = unit_tokens(unit)
+            stage_v = stage_of[unit // GROUP_UNITS][1]
+            nc.vector.tensor_tensor(
+                out=stage_v[:, :, tokens, :],
+                in0=scaled_of[unit][:].rearrange("p t (h j) -> p h t j", h=HEADS),
+                in1=affine_rows[:, 1, :]
+                .rearrange("p (h j) -> p h j", h=HEADS)
+                .unsqueeze(2)
+                .to_broadcast([P, HEADS, UNIT_TOKENS, V_DIM]),
+                op=ALU.add,
+            )
 
         def store(group):
             stage_qk, stage_v = stage_of[group]
@@ -255,10 +329,20 @@ def tile_attention_pa_t_kernel(tc, x, qkv_w, qkv_g, qkv_b, out_q, out_k, out_v):
                         in_=rows.rearrange("p h t j -> p h (t j)"),
                     )
 
-        for step in range(UNITS + LAG):
-            if step < UNITS:
-                normalise(step)
-            if step >= LAG:
-                collect(step - LAG)
-                if (step - LAG) % GROUP_UNITS == GROUP_UNITS - 1:
-                    store((step - LAG) // GROUP_UNITS)
+        normalise_qk(order[0])
+        scale_v(order[0])
+        for step in range(UNITS):
+            unit = order[step]
+            if step + 1 < UNITS:
+                normalise_qk(order[step + 1])
+                scale_v(order[step + 1])
+            if unit % GROUP_UNITS == 0:
+                open_stages(unit // GROUP_UNITS)
+            collect_qk(unit)
+            shift_v(unit)
+            if step + LAG + 1 < UNITS:
+                ahead = order[step + LAG + 1]
+                y_qk[ahead] = multiply(ahead, 0)
+                y_v[ahead] = multiply_rows(ahead, 1)
+            if unit % GROUP_UNITS == GROUP_UNITS - 1:
+                store(unit // GROUP_UNITS)

@@ -17,6 +17,7 @@ HEADS, QK_DIM, V_DIM = 4, 16, 32
 HEAD_FEATURES = 2 * QK_DIM + V_DIM
 FEATURES = HEADS * HEAD_FEATURES
 HALVES = FEATURES // P
+QK, V = 0, 1
 ROWS = BATCHES * TOKENS
 EPS = 1e-5
 
@@ -25,20 +26,17 @@ WORDS = CHANNELS // 2
 WORD_PLANES = WORDS // P
 
 BANK = 512
+BLOCK = 32
 UNIT_TOKENS = BANK // P
-GROUP_TOKENS = 8
-GROUP_UNITS = GROUP_TOKENS // UNIT_TOKENS
-GROUP_BATCHES = P * GROUP_TOKENS // TOKENS
-RUNS = TOKENS // GROUP_TOKENS
+TOKENS_PER_BANK = BANK // WORDS
+RUN_TOKENS = TOKENS // BLOCK
+GROUP_BATCHES = P // BLOCK
+GROUP_UNITS = RUN_TOKENS // UNIT_TOKENS
+GROUP_COLS = GROUP_UNITS * BANK
 UNITS = ROWS // BANK
+GROUPS = UNITS // GROUP_UNITS
 BN_STATS_DIM = 6
 LAG = 2
-
-PARTS = (
-    (0, QK_DIM, 0),
-    (QK_DIM, QK_DIM, HEADS * QK_DIM),
-    (2 * QK_DIM, V_DIM, 2 * HEADS * QK_DIM),
-)
 
 FLOPS = 2 * ROWS * CHANNELS * FEATURES
 
@@ -49,19 +47,18 @@ def tile_attention_pa_t_kernel(tc, x, qkv_w, qkv_g, qkv_b, out_q, out_k, out_v):
         const = ctx.enter_context(tc.tile_pool(name="const", bufs=1))
         x_pool = ctx.enter_context(tc.tile_pool(name="x_rows", bufs=UNITS))
         grouped_pool = ctx.enter_context(tc.tile_pool(name="grouped", bufs=3))
-        zt_pool = ctx.enter_context(tc.tile_pool(name="zt", bufs=3))
-        scaled_pool = ctx.enter_context(tc.tile_pool(name="scaled", bufs=3))
-        stage_pool = ctx.enter_context(tc.tile_pool(name="stage", bufs=3))
+        z_pool = ctx.enter_context(tc.tile_pool(name="z", bufs=2))
+        stage_pool = ctx.enter_context(tc.tile_pool(name="stage", bufs=4))
         psum = ctx.enter_context(tc.psum_pool(name="psum", bufs=8))
         ctx.enter_context(tc.manual_schedule())
 
-        gb_rows = const.tile([P, FEATURES], BF16)
-        nc.gpsimd.memset(gb_rows[:], 0.0)
         w_rows = const.tile([P, HALVES * CHANNELS], BF16)
         nc.sync.dma_start(
             out=w_rows[:].rearrange("p (s k) -> p s k", s=HALVES),
             in_=qkv_w.rearrange("(s p) k -> p s k", s=HALVES),
         )
+        gb_rows = const.tile([P, FEATURES], BF16)
+        nc.gpsimd.memset(gb_rows[:], 0.0)
         x_units = x.flatten_outer_dims().rearrange(
             "(g p s t) k -> g s p (t k)", p=P, s=GROUP_UNITS, t=UNIT_TOKENS
         )
@@ -83,14 +80,8 @@ def tile_attention_pa_t_kernel(tc, x, qkv_w, qkv_g, qkv_b, out_q, out_k, out_v):
         nc.vector.memset(one[:], 1.0)
         table_warm = const.tile([P, 1], F32)
         nc.scalar.activation(out=table_warm[:], in_=one[:], func=ACT.Sqrt)
-
         identity = const.tile([P, P], F32)
         make_identity(nc, identity[:])
-        row_order = const.tile([P, P], F32)
-        nc.vector.tensor_copy(
-            out=row_order[:].rearrange("p (r b) -> p r b", b=GROUP_BATCHES),
-            in_=identity[:].rearrange("p (b r) -> p r b", b=GROUP_BATCHES),
-        )
 
         w_words = w_rows[:].bitcast(F32)
         wt = psum.tile([P, HALVES, WORD_PLANES, P], F32, tag="bank")
@@ -99,17 +90,16 @@ def tile_attention_pa_t_kernel(tc, x, qkv_w, qkv_g, qkv_b, out_q, out_k, out_v):
                 words_u = slice(s * WORDS + u, (s + 1) * WORDS, WORD_PLANES)
                 nc.tensor.transpose(wt[:, s, u, :], w_words[:, words_u], identity[:])
         w_grouped = const.tile([P, FEATURES * PACK], BF16, align_bytes=64)
-        w_grouped_words = w_grouped[:].bitcast(F32).rearrange("p (f u) -> p f u", u=WORD_PLANES)
+        w_by_half = w_grouped[:].bitcast(F32).rearrange(
+            "p (half h j u) -> p half h j u", half=HALVES, h=HEADS, u=WORD_PLANES
+        )
         heads_here = HEADS // HALVES
         for s in range(HALVES):
-            by_head = wt[:, s].rearrange("p u (h j) -> p h j u", h=heads_here)
-            for first, width, base in PARTS:
-                start = base + s * heads_here * width
+            by_head = wt[:, s].rearrange("p u (h half j) -> p half h j u", h=heads_here, half=HALVES)
+            for half in range(HALVES):
                 nc.vector.tensor_copy(
-                    out=w_grouped_words[:, start : start + heads_here * width, :].rearrange(
-                        "p (h j) u -> p h j u", h=heads_here
-                    ),
-                    in_=by_head[:, :, first : first + width, :],
+                    out=w_by_half[:, half, s * heads_here : (s + 1) * heads_here],
+                    in_=by_head[:, half],
                 )
         w_codes = const.tile([P, FEATURES], U32, align_bytes=64)
         w_scales = const.tile([P, FEATURES], U8, align_bytes=64)
@@ -119,13 +109,10 @@ def tile_attention_pa_t_kernel(tc, x, qkv_w, qkv_g, qkv_b, out_q, out_k, out_v):
         gain_shift = const.tile([P, HALVES, 2], F32)
 
         def sort_gain_shift():
-            gb_by_head = gb_rows[:].rearrange("p (h j) -> p h j", h=HEADS)
-            for first, width, base in PARTS:
+            for half in range(HALVES):
                 nc.vector.tensor_copy(
-                    out=gb_sorted[:, base : base + HEADS * width].rearrange(
-                        "p (h j) -> p h j", h=HEADS
-                    ),
-                    in_=gb_by_head[:, :, first : first + width],
+                    out=gb_sorted[:, half * P : (half + 1) * P].rearrange("p (h j) -> p h j", h=HEADS),
+                    in_=gb_rows[:].rearrange("p (h half j) -> p half h j", h=HEADS, half=HALVES)[:, half],
                 )
 
         def turn_gain_shift():
@@ -139,39 +126,27 @@ def tile_attention_pa_t_kernel(tc, x, qkv_w, qkv_g, qkv_b, out_q, out_k, out_v):
         x_codes = const.tile([P, ROWS], U32, align_bytes=64)
         x_scales = const.tile([P, ROWS], U8, align_bytes=64)
 
-        def multiply(unit, half):
+        def multiply(unit):
             cols = slice(unit * BANK, (unit + 1) * BANK)
-            features = slice(half * P, (half + 1) * P)
-            y = psum.tile([P, BANK], F32, tag="bank")
-            nc.tensor.matmul_mx(
-                out=y[:],
-                lhsT=w_codes[:, features].bitcast(FP8X4),
-                lhsT_scale=w_scales[:, features],
-                rhs=x_codes[:, cols].bitcast(FP8X4),
-                rhs_scale=x_scales[:, cols],
-                start=True,
-                stop=True,
-            )
-            return y
-
-        def multiply_rows(unit, half):
-            features = slice(half * P, (half + 1) * P)
-            y = psum.tile([P, UNIT_TOKENS, P], F32, tag="bank")
-            for t in range(UNIT_TOKENS):
-                rows = slice(unit * BANK + t * P, unit * BANK + (t + 1) * P)
+            banks = []
+            for half in range(HALVES):
+                features = slice(half * P, (half + 1) * P)
+                y = psum.tile([P, BANK], F32, tag="bank")
                 nc.tensor.matmul_mx(
-                    out=y[:, t, :],
-                    lhsT=x_codes[:, rows].bitcast(FP8X4),
-                    lhsT_scale=x_scales[:, rows],
-                    rhs=w_codes[:, features].bitcast(FP8X4),
-                    rhs_scale=w_scales[:, features],
+                    out=y[:],
+                    lhsT=w_codes[:, features].bitcast(FP8X4),
+                    lhsT_scale=w_scales[:, features],
+                    rhs=x_codes[:, cols].bitcast(FP8X4),
+                    rhs_scale=x_scales[:, cols],
                     start=True,
                     stop=True,
                 )
-            return y
+                banks.append(y)
+            return banks
 
         stats = const.tile([P, HALVES, UNITS, BN_STATS_DIM], F32)
         grouped_of = {}
+        banks_of = {}
 
         def transpose_x(unit):
             words = x_rows[unit][:].bitcast(F32)
@@ -179,16 +154,15 @@ def tile_attention_pa_t_kernel(tc, x, qkv_w, qkv_g, qkv_b, out_q, out_k, out_v):
             grouped_words = grouped[:].bitcast(F32).rearrange(
                 "p (t c u) -> p t c u", t=UNIT_TOKENS, u=WORD_PLANES
             )
-            tokens_per_bank = BANK // WORDS
-            for first_token in range(0, UNIT_TOKENS, tokens_per_bank):
-                xt = psum.tile([P, tokens_per_bank, WORD_PLANES, P], F32, tag="bank")
-                for t in range(tokens_per_bank):
+            for first_token in range(0, UNIT_TOKENS, TOKENS_PER_BANK):
+                xt = psum.tile([P, TOKENS_PER_BANK, WORD_PLANES, P], F32, tag="bank")
+                for t in range(TOKENS_PER_BANK):
                     for u in range(WORD_PLANES):
                         token = first_token + t
                         words_u = slice(token * WORDS + u, (token + 1) * WORDS, WORD_PLANES)
-                        nc.tensor.transpose(xt[:, t, u, :], words[:, words_u], row_order[:])
+                        nc.tensor.transpose(xt[:, t, u, :], words[:, words_u], identity[:])
                 nc.scalar.copy(
-                    out=grouped_words[:, first_token : first_token + tokens_per_bank],
+                    out=grouped_words[:, first_token : first_token + TOKENS_PER_BANK],
                     in_=xt[:].rearrange("p t u c -> p t c u"),
                 )
             grouped_of[unit] = grouped
@@ -201,10 +175,8 @@ def tile_attention_pa_t_kernel(tc, x, qkv_w, qkv_g, qkv_b, out_q, out_k, out_v):
                 in_=grouped_of[unit][:],
             )
 
-        banks_of = {}
-
         def measure(unit):
-            banks_of[unit] = [multiply(unit, half) for half in range(HALVES)]
+            banks_of[unit] = multiply(unit)
             for half, y in enumerate(banks_of[unit]):
                 nc.vector.bn_stats(out=stats[:, half, unit, :], in_=y[:])
 
@@ -220,13 +192,13 @@ def tile_attention_pa_t_kernel(tc, x, qkv_w, qkv_g, qkv_b, out_q, out_k, out_v):
             if step == UNITS // 2 + 1:
                 turn_gain_shift()
 
-        order = list(range(UNITS - LAG, UNITS)) + list(range(UNITS - LAG))
-        y_qk = {unit: banks_of[unit][0] for unit in order[:LAG]}
-        y_v = {}
-        affine_bank = psum.tile([P, 2, P], F32, tag="bank")
-        for unit in order[:LAG]:
-            y_v[unit] = multiply_rows(unit, 1)
-        y_qk[order[LAG]] = multiply(order[LAG], 0)
+        order = [GROUPS - 1] + list(range(GROUPS - 1))
+
+        def multiply_group(group):
+            for unit in range(group * GROUP_UNITS, (group + 1) * GROUP_UNITS):
+                banks_of[unit] = multiply(unit)
+
+        multiply_group(order[1])
 
         mean_var = const.tile([P, HALVES, 2], F32)
         for half in range(HALVES):
@@ -250,99 +222,68 @@ def tile_attention_pa_t_kernel(tc, x, qkv_w, qkv_g, qkv_b, out_q, out_k, out_v):
             out=shift[:], in0=gain_shift[:, :, 1], in1=mean_scaled[:], op=ALU.subtract
         )
 
-        for i, column in enumerate((scale, shift)):
-            nc.tensor.matmul(
-                affine_bank[:, i, :],
-                lhsT=column[:, 1:2].to_broadcast([P, P]),
-                rhs=identity[:],
-                start=True,
-                stop=True,
-            )
-        affine_rows = const.tile([P, 2, P], F32)
-        nc.vector.tensor_copy(out=affine_rows[:], in_=affine_bank[:])
-        y_v[order[LAG]] = multiply_rows(order[LAG], 1)
-
-        zt_of = {}
-        scaled_of = {}
-        stage_of = {}
-
-        def normalise_qk(unit):
-            zt = zt_pool.tile([P, BANK], F32)
-            nc.scalar.activation(
-                out=zt[:], in_=y_qk[unit][:], func=ACT.Identity, bias=shift[:, 0:1], scale=scale[:, 0:1]
-            )
-            zt_of[unit] = zt
-
-        def scale_v(unit):
-            scaled = scaled_pool.tile([P, UNIT_TOKENS, P], F32)
-            nc.vector.tensor_tensor(
-                out=scaled[:],
-                in0=y_v[unit][:],
-                in1=affine_rows[:, 0:1, :].to_broadcast([P, UNIT_TOKENS, P]),
-                op=ALU.mult,
-            )
-            scaled_of[unit] = scaled
-
-        def open_stages(group):
-            stage_qk = stage_pool.tile([P, 2 * HEADS, GROUP_TOKENS, QK_DIM], F32)
-            stage_v = stage_pool.tile([P, HEADS, GROUP_TOKENS, V_DIM], F32)
-            stage_of[group] = (stage_qk, stage_v)
-
-        def unit_tokens(unit):
+        def normalise(z, unit, half, on_vector=False):
             part = unit % GROUP_UNITS
-            return slice(part * UNIT_TOKENS, (part + 1) * UNIT_TOKENS)
+            tokens = slice(part * UNIT_TOKENS, (part + 1) * UNIT_TOKENS)
+            out = z[:].rearrange("p (b t r) -> p t b r", b=GROUP_BATCHES, r=BLOCK)[:, tokens]
+            y = banks_of[unit][half][:].rearrange("p (t b r) -> p t b r", b=GROUP_BATCHES, r=BLOCK)
+            scale_col = scale[:, half : half + 1]
+            shift_col = shift[:, half : half + 1]
+            if on_vector:
+                nc.vector.tensor_scalar(
+                    out=out, in0=y, scalar1=scale_col, scalar2=shift_col, op0=ALU.mult, op1=ALU.add
+                )
+            else:
+                nc.scalar.activation(out=out, in_=y, func=ACT.Identity, bias=shift_col, scale=scale_col)
 
-        def collect_qk(unit):
-            tokens = unit_tokens(unit)
-            stage_qk = stage_of[unit // GROUP_UNITS][0]
-            z = psum.tile([P, UNIT_TOKENS, P], F32, tag="bank")
-            for t in range(UNIT_TOKENS):
-                nc.tensor.transpose(z[:, t, :], zt_of[unit][:, t * P : (t + 1) * P], identity[:])
-            nc.scalar.copy(
-                out=stage_qk[:, :, tokens, :], in_=z[:].rearrange("p t (a j) -> p a t j", j=QK_DIM)
+        def store(out, stage, group, first=0, batches=GROUP_BATCHES):
+            batch = group * GROUP_BATCHES + first
+            nc.sync.dma_start(
+                out=out[batch : batch + batches].rearrange("b h (r t) j -> (h r) b (t j)", t=RUN_TOKENS),
+                in_=stage.rearrange("p (b c) -> p b c", b=batches),
             )
 
-        def shift_v(unit):
-            tokens = unit_tokens(unit)
-            stage_v = stage_of[unit // GROUP_UNITS][1]
-            nc.vector.tensor_tensor(
-                out=stage_v[:, :, tokens, :],
-                in0=scaled_of[unit][:].rearrange("p t (h j) -> p h t j", h=HEADS),
-                in1=affine_rows[:, 1, :]
-                .rearrange("p (h j) -> p h j", h=HEADS)
-                .unsqueeze(2)
-                .to_broadcast([P, HEADS, UNIT_TOKENS, V_DIM]),
-                op=ALU.add,
+        def finish_v(z, group, pieces):
+            stage = stage_pool.tile([P, GROUP_COLS], F32, align_bytes=64, name="stage_v")
+            width = GROUP_COLS // pieces
+            batches = GROUP_BATCHES // pieces
+            for piece in range(pieces):
+                cols = slice(piece * width, (piece + 1) * width)
+                nc.vector.transpose(stage[:, cols], z[:, cols])
+                store(out_v, stage[:, cols], group, piece * batches, batches)
+
+        def finish_qk(z, group):
+            turned = z_pool.tile([P, GROUP_COLS], F32, align_bytes=64, name="turned")
+            nc.vector.transpose(turned[:], z[:])
+            stage = stage_pool.tile([P, 2, GROUP_COLS // 2], F32, name="stage_qk")
+            nc.gpsimd.tensor_scalar(
+                out=stage[:].rearrange("p e (c j) -> p c e j", j=QK_DIM),
+                in0=turned[:].rearrange("p (c e j) -> p c e j", e=2, j=QK_DIM),
+                scalar1=1.0,
+                scalar2=0.0,
+                op0=ALU.mult,
+                op1=ALU.add,
             )
+            store(out_q, stage[:, 0], group)
+            store(out_k, stage[:, 1], group)
 
-        def store(group):
-            stage_qk, stage_v = stage_of[group]
-            for b in range(GROUP_BATCHES):
-                batch = group * GROUP_BATCHES + b
-                for out, rows in (
-                    (out_q, stage_qk[b:P:GROUP_BATCHES, 0:HEADS]),
-                    (out_k, stage_qk[b:P:GROUP_BATCHES, HEADS : 2 * HEADS]),
-                    (out_v, stage_v[b:P:GROUP_BATCHES]),
-                ):
-                    nc.sync.dma_start(
-                        out=out[batch].rearrange("h (r t) j -> r h (t j)", t=GROUP_TOKENS),
-                        in_=rows.rearrange("p h t j -> p h (t j)"),
-                    )
-
-        normalise_qk(order[0])
-        scale_v(order[0])
-        for step in range(UNITS):
-            unit = order[step]
-            if step + 1 < UNITS:
-                normalise_qk(order[step + 1])
-                scale_v(order[step + 1])
-            if unit % GROUP_UNITS == 0:
-                open_stages(unit // GROUP_UNITS)
-            collect_qk(unit)
-            shift_v(unit)
-            if step + LAG + 1 < UNITS:
-                ahead = order[step + LAG + 1]
-                y_qk[ahead] = multiply(ahead, 0)
-                y_v[ahead] = multiply_rows(ahead, 1)
-            if unit % GROUP_UNITS == GROUP_UNITS - 1:
-                store(unit // GROUP_UNITS)
+        for step, group in enumerate(order):
+            first, second = range(group * GROUP_UNITS, (group + 1) * GROUP_UNITS)
+            z_qk = z_pool.tile([P, GROUP_COLS], F32, align_bytes=64, name="z_qk")
+            z_v = z_pool.tile([P, GROUP_COLS], F32, align_bytes=64, name="z_v")
+            if step == 0:
+                normalise(z_v, first, V)
+                normalise(z_v, second, V, on_vector=True)
+                finish_v(z_v, group, 2)
+                normalise(z_qk, first, QK)
+                normalise(z_qk, second, QK)
+                finish_qk(z_qk, group)
+            else:
+                normalise(z_qk, first, QK)
+                normalise(z_qk, second, QK)
+                finish_qk(z_qk, group)
+                normalise(z_v, first, V)
+                normalise(z_v, second, V)
+                finish_v(z_v, group, 2 if step == GROUPS - 1 else 1)
+            if step + 2 < GROUPS:
+                multiply_group(order[step + 2])

@@ -29,13 +29,17 @@ BANK = 512
 BLOCK = 32
 UNIT_TOKENS = BANK // P
 TOKENS_PER_BANK = BANK // WORDS
-RUN_TOKENS = TOKENS // BLOCK
-GROUP_BATCHES = P // BLOCK
-GROUP_UNITS = RUN_TOKENS // UNIT_TOKENS
+UNIT_BATCHES = BANK // TOKENS
+RUNS = BLOCK // UNIT_BATCHES
+RUN_TOKENS = TOKENS // RUNS
+PARTS = RUN_TOKENS // UNIT_TOKENS
+GROUP_UNITS = 2
+GROUP_BATCHES = GROUP_UNITS * UNIT_BATCHES
 GROUP_COLS = GROUP_UNITS * BANK
 UNITS = ROWS // BANK
 GROUPS = UNITS // GROUP_UNITS
 BN_STATS_DIM = 6
+SCALAR_UNITS = range(1, 13, 3)
 LAG = 2
 
 FLOPS = 2 * ROWS * CHANNELS * FEATURES
@@ -47,30 +51,31 @@ def tile_attention_pa_t_kernel(tc, x, qkv_w, qkv_g, qkv_b, out_q, out_k, out_v):
         const = ctx.enter_context(tc.tile_pool(name="const", bufs=1))
         x_pool = ctx.enter_context(tc.tile_pool(name="x_rows", bufs=UNITS))
         grouped_pool = ctx.enter_context(tc.tile_pool(name="grouped", bufs=3))
+        unused_pool = ctx.enter_context(tc.tile_pool(name="unused", bufs=2))
         z_pool = ctx.enter_context(tc.tile_pool(name="z", bufs=2))
         stage_pool = ctx.enter_context(tc.tile_pool(name="stage", bufs=4))
-        psum = ctx.enter_context(tc.psum_pool(name="psum", bufs=8))
+        psum_t = ctx.enter_context(tc.psum_pool(name="psum_t", bufs=4))
+        psum_y = ctx.enter_context(tc.psum_pool(name="psum_y", bufs=4))
         ctx.enter_context(tc.manual_schedule())
 
         w_rows = const.tile([P, HALVES * CHANNELS], BF16)
-        nc.sync.dma_start(
-            out=w_rows[:].rearrange("p (s k) -> p s k", s=HALVES),
-            in_=qkv_w.rearrange("(s p) k -> p s k", s=HALVES),
-        )
         gb_rows = const.tile([P, FEATURES], BF16)
         nc.gpsimd.memset(gb_rows[:], 0.0)
-        x_units = x.flatten_outer_dims().rearrange(
-            "(g p s t) k -> g s p (t k)", p=P, s=GROUP_UNITS, t=UNIT_TOKENS
-        )
+        x_units = x.flatten_outer_dims().rearrange("(n p t) k -> n p (t k)", p=P, t=UNIT_TOKENS)
         x_rows = []
         for unit in range(UNITS):
             x_tile = x_pool.tile([P, UNIT_TOKENS * CHANNELS], BF16, name="x_tile")
-            source = x_units[unit // GROUP_UNITS, unit % GROUP_UNITS]
-            pieces = 2 if unit == 0 else 1
+            source = x_units[unit]
+            pieces = UNIT_TOKENS // TOKENS_PER_BANK if unit == 0 else 1
             width = UNIT_TOKENS * CHANNELS // pieces
             for piece in range(pieces):
                 cols = slice(piece * width, (piece + 1) * width)
                 nc.sync.dma_start(out=x_tile[:, cols], in_=source[:, cols])
+                if unit == 0 and piece == 0:
+                    nc.sync.dma_start(
+                        out=w_rows[:].rearrange("p (s k) -> p s k", s=HALVES),
+                        in_=qkv_w.rearrange("(s p) k -> p s k", s=HALVES),
+                    )
             x_rows.append(x_tile)
             if unit == 3:
                 nc.sync.dma_start(out=gb_rows[0:1, :], in_=qkv_g.rearrange("(o f) -> o f", o=1))
@@ -79,34 +84,47 @@ def tile_attention_pa_t_kernel(tc, x, qkv_w, qkv_g, qkv_b, out_q, out_k, out_v):
         one = const.tile([P, 1], F32)
         nc.vector.memset(one[:], 1.0)
         table_warm = const.tile([P, 1], F32)
-        nc.scalar.activation(out=table_warm[:], in_=one[:], func=ACT.Sqrt)
+        nc.scalar.activation(out=table_warm[:], in_=one[:], func=ACT.Abs_reciprocal_sqrt)
+        eps = const.tile([P, 1], F32)
+        nc.vector.memset(eps[:], 0.0)
+        nc.vector.tensor_scalar(out=eps[:], in0=eps[:], scalar1=EPS, scalar2=None, op0=ALU.add)
         identity = const.tile([P, P], F32)
         make_identity(nc, identity[:])
-
-        w_words = w_rows[:].bitcast(F32)
-        wt = psum.tile([P, HALVES, WORD_PLANES, P], F32, tag="bank")
-        for s in range(HALVES):
-            for u in range(WORD_PLANES):
-                words_u = slice(s * WORDS + u, (s + 1) * WORDS, WORD_PLANES)
-                nc.tensor.transpose(wt[:, s, u, :], w_words[:, words_u], identity[:])
-        w_grouped = const.tile([P, FEATURES * PACK], BF16, align_bytes=64)
-        w_by_half = w_grouped[:].bitcast(F32).rearrange(
-            "p (half h j u) -> p half h j u", half=HALVES, h=HEADS, u=WORD_PLANES
+        row_order = const.tile([P, P], F32)
+        nc.vector.tensor_copy(
+            out=row_order[:].rearrange("p (s r c) -> p s r c", r=RUNS, c=UNIT_BATCHES),
+            in_=identity[:].rearrange("p (c r s) -> p s r c", r=RUNS, c=UNIT_BATCHES),
         )
-        heads_here = HEADS // HALVES
-        for s in range(HALVES):
-            by_head = wt[:, s].rearrange("p u (h half j) -> p half h j u", h=heads_here, half=HALVES)
-            for half in range(HALVES):
-                nc.vector.tensor_copy(
-                    out=w_by_half[:, half, s * heads_here : (s + 1) * heads_here],
-                    in_=by_head[:, half],
-                )
+
         w_codes = const.tile([P, FEATURES], U32, align_bytes=64)
         w_scales = const.tile([P, FEATURES], U8, align_bytes=64)
-        nc.vector.quantize_mx(out=w_codes[:].bitcast(FP8X4), scales=w_scales[:], in_=w_grouped[:])
+
+        def prepare_weights():
+            w_words = w_rows[:].bitcast(F32)
+            wt = psum_t.tile([P, HALVES, WORD_PLANES, P], F32, tag="bank")
+            for s in range(HALVES):
+                for u in range(WORD_PLANES):
+                    words_u = slice(s * WORDS + u, (s + 1) * WORDS, WORD_PLANES)
+                    nc.tensor.transpose(wt[:, s, u, :], w_words[:, words_u], identity[:])
+            w_grouped = const.tile([P, FEATURES * PACK], BF16, align_bytes=64)
+            w_by_half = w_grouped[:].bitcast(F32).rearrange(
+                "p (half h j u) -> p half h j u", half=HALVES, h=HEADS, u=WORD_PLANES
+            )
+            heads_here = HEADS // HALVES
+            for s in range(HALVES):
+                by_head = wt[:, s].rearrange("p u (h half j) -> p half h j u", h=heads_here, half=HALVES)
+                for half in range(HALVES):
+                    nc.vector.tensor_copy(
+                        out=w_by_half[:, half, s * heads_here : (s + 1) * heads_here],
+                        in_=by_head[:, half],
+                    )
+            nc.vector.quantize_mx(
+                out=w_codes[:].bitcast(FP8X4), scales=w_scales[:], in_=w_grouped[:]
+            )
 
         gb_sorted = const.tile([P, FEATURES], F32)
         gain_shift = const.tile([P, HALVES, 2], F32)
+        minus_gain = const.tile([P, HALVES], F32)
 
         def sort_gain_shift():
             for half in range(HALVES):
@@ -116,17 +134,20 @@ def tile_attention_pa_t_kernel(tc, x, qkv_w, qkv_g, qkv_b, out_q, out_k, out_v):
                 )
 
         def turn_gain_shift():
-            gb_t = psum.tile([P, HALVES, P], F32, tag="bank")
+            gb_t = psum_t.tile([P, HALVES, P], F32, tag="bank")
             for half in range(HALVES):
                 nc.tensor.transpose(
                     gb_t[:, half, :], gb_sorted[:, half * P : (half + 1) * P], identity[:]
                 )
             nc.vector.tensor_copy(out=gain_shift[:], in_=gb_t[:, :, 0:2])
+            nc.gpsimd.tensor_scalar(
+                out=minus_gain[:], in0=gain_shift[:, :, 0], scalar1=-1.0, scalar2=None, op0=ALU.mult
+            )
 
         x_codes = const.tile([P, ROWS], U32, align_bytes=64)
         x_scales = const.tile([P, ROWS], U8, align_bytes=64)
 
-        def multiply(unit):
+        def multiply(unit, psum):
             cols = slice(unit * BANK, (unit + 1) * BANK)
             banks = []
             for half in range(HALVES):
@@ -145,6 +166,9 @@ def tile_attention_pa_t_kernel(tc, x, qkv_w, qkv_g, qkv_b, out_q, out_k, out_v):
             return banks
 
         stats = const.tile([P, HALVES, UNITS, BN_STATS_DIM], F32)
+        minus_center = const.tile([P, 1], F32)
+        sums = const.tile([P, len(SCALAR_UNITS)], F32)
+        squares = const.tile([P, len(SCALAR_UNITS)], F32)
         grouped_of = {}
         banks_of = {}
 
@@ -155,16 +179,18 @@ def tile_attention_pa_t_kernel(tc, x, qkv_w, qkv_g, qkv_b, out_q, out_k, out_v):
                 "p (t c u) -> p t c u", t=UNIT_TOKENS, u=WORD_PLANES
             )
             for first_token in range(0, UNIT_TOKENS, TOKENS_PER_BANK):
-                xt = psum.tile([P, TOKENS_PER_BANK, WORD_PLANES, P], F32, tag="bank")
+                xt = psum_t.tile([P, TOKENS_PER_BANK, WORD_PLANES, P], F32, tag="bank")
                 for t in range(TOKENS_PER_BANK):
                     for u in range(WORD_PLANES):
                         token = first_token + t
                         words_u = slice(token * WORDS + u, (token + 1) * WORDS, WORD_PLANES)
-                        nc.tensor.transpose(xt[:, t, u, :], words[:, words_u], identity[:])
+                        nc.tensor.transpose(xt[:, t, u, :], words[:, words_u], row_order[:])
                 nc.scalar.copy(
                     out=grouped_words[:, first_token : first_token + TOKENS_PER_BANK],
                     in_=xt[:].rearrange("p t u c -> p t c u"),
                 )
+                if unit == 0 and first_token == 0:
+                    prepare_weights()
             grouped_of[unit] = grouped
 
         def quantise_x(unit):
@@ -176,17 +202,74 @@ def tile_attention_pa_t_kernel(tc, x, qkv_w, qkv_g, qkv_b, out_q, out_k, out_v):
             )
 
         def measure(unit):
-            banks_of[unit] = multiply(unit)
+            banks_of[unit] = multiply(unit, psum_y)
             for half, y in enumerate(banks_of[unit]):
-                nc.vector.bn_stats(out=stats[:, half, unit, :], in_=y[:])
+                if not (half == QK and unit in SCALAR_UNITS):
+                    nc.vector.bn_stats(out=stats[:, half, unit, :], in_=y[:])
+            if unit == 0:
+                nc.gpsimd.tensor_scalar(
+                    out=minus_center[:], in0=stats[:, QK, 0, 1:2], scalar1=-1.0, scalar2=None, op0=ALU.mult
+                )
+
+        def measure_on_scalar(unit, func, total):
+            i = SCALAR_UNITS.index(unit)
+            unused = unused_pool.tile([P, BANK], BF16)
+            nc.scalar.activation(
+                out=unused[:],
+                in_=banks_of[unit][QK][:],
+                func=func,
+                bias=minus_center[:],
+                accum_out=total[:, i : i + 1],
+            )
+
+        def join_scalar_units():
+            count = len(SCALAR_UNITS)
+            offset = const.tile([P, count], F32)
+            nc.gpsimd.tensor_scalar(
+                out=offset[:], in0=sums[:], scalar1=1.0 / BANK, scalar2=None, op0=ALU.mult
+            )
+            spread = const.tile([P, count], F32)
+            nc.gpsimd.tensor_tensor(out=spread[:], in0=offset[:], in1=sums[:], op=ALU.mult)
+            nc.gpsimd.tensor_tensor(out=spread[:], in0=squares[:], in1=spread[:], op=ALU.subtract)
+            joined = const.tile([P, count, BN_STATS_DIM], F32)
+            nc.gpsimd.memset(joined[:], BANK / 2)
+            for part in range(2):
+                nc.gpsimd.tensor_scalar(
+                    out=joined[:, :, 3 * part + 1],
+                    in0=offset[:],
+                    scalar1=minus_center[:],
+                    scalar2=None,
+                    op0=ALU.subtract,
+                )
+                nc.gpsimd.tensor_scalar(
+                    out=joined[:, :, 3 * part + 2],
+                    in0=spread[:],
+                    scalar1=0.5,
+                    scalar2=None,
+                    op0=ALU.mult,
+                )
+            return joined
 
         for step in range(UNITS + LAG):
             if step < UNITS:
                 transpose_x(step)
             if 1 <= step <= UNITS:
                 quantise_x(step - 1)
-            if step >= LAG:
+            if step == 1:
+                measure(0)
+            if step > LAG:
                 measure(step - LAG)
+            if step - LAG in SCALAR_UNITS:
+                measure_on_scalar(step - LAG, ACT.Identity, sums)
+            if step - LAG - 1 in SCALAR_UNITS:
+                measure_on_scalar(step - LAG - 1, ACT.Square, squares)
+            if step - LAG - 1 == SCALAR_UNITS[-1]:
+                joined = join_scalar_units()
+            if step == UNITS:
+                nc.vector.tensor_copy(
+                    out=stats[:, QK, SCALAR_UNITS.start : SCALAR_UNITS.stop : SCALAR_UNITS.step, :],
+                    in_=joined[:],
+                )
             if step == UNITS // 2:
                 sort_gain_shift()
             if step == UNITS // 2 + 1:
@@ -194,39 +277,43 @@ def tile_attention_pa_t_kernel(tc, x, qkv_w, qkv_g, qkv_b, out_q, out_k, out_v):
 
         order = [GROUPS - 1] + list(range(GROUPS - 1))
 
-        def multiply_group(group):
+        def multiply_group(step):
+            group = order[step]
             for unit in range(group * GROUP_UNITS, (group + 1) * GROUP_UNITS):
-                banks_of[unit] = multiply(unit)
+                banks_of[unit] = multiply(unit, psum_t if step % 2 else psum_y)
 
-        multiply_group(order[1])
+        multiply_group(1)
 
         mean_var = const.tile([P, HALVES, 2], F32)
         for half in range(HALVES):
             nc.vector.bn_aggr(
                 out=mean_var[:, half, :], in_=stats[:, half].rearrange("p u s -> p (u s)")
             )
-        var_eps = const.tile([P, HALVES], F32)
-        nc.vector.tensor_scalar(
-            out=var_eps[:], in0=mean_var[:, :, 1], scalar1=EPS, scalar2=None, op0=ALU.add
-        )
-        std = const.tile([P, HALVES], F32)
-        nc.scalar.activation(out=std[:], in_=var_eps[:], func=ACT.Sqrt)
         inv_std = const.tile([P, HALVES], F32)
-        nc.vector.reciprocal(out=inv_std[:], in_=std[:])
+        nc.scalar.activation(
+            out=inv_std[:], in_=mean_var[:, :, 1], func=ACT.Abs_reciprocal_sqrt, bias=eps[:]
+        )
+        mean_gain = const.tile([P, HALVES], F32)
+        nc.vector.tensor_tensor(
+            out=mean_gain[:], in0=mean_var[:, :, 0], in1=minus_gain[:], op=ALU.mult
+        )
         scale = const.tile([P, HALVES], F32)
         nc.vector.tensor_tensor(out=scale[:], in0=gain_shift[:, :, 0], in1=inv_std[:], op=ALU.mult)
-        mean_scaled = const.tile([P, HALVES], F32)
-        nc.vector.tensor_tensor(out=mean_scaled[:], in0=mean_var[:, :, 0], in1=scale[:], op=ALU.mult)
         shift = const.tile([P, HALVES], F32)
-        nc.vector.tensor_tensor(
-            out=shift[:], in0=gain_shift[:, :, 1], in1=mean_scaled[:], op=ALU.subtract
-        )
+        for half in (V, QK):
+            nc.vector.scalar_tensor_tensor(
+                out=shift[:, half : half + 1],
+                in0=mean_gain[:, half : half + 1],
+                scalar=inv_std[:, half : half + 1],
+                in1=gain_shift[:, half, 1:2],
+                op0=ALU.mult,
+                op1=ALU.add,
+            )
 
         def normalise(z, unit, half, on_vector=False):
             part = unit % GROUP_UNITS
-            tokens = slice(part * UNIT_TOKENS, (part + 1) * UNIT_TOKENS)
-            out = z[:].rearrange("p (b t r) -> p t b r", b=GROUP_BATCHES, r=BLOCK)[:, tokens]
-            y = banks_of[unit][half][:].rearrange("p (t b r) -> p t b r", b=GROUP_BATCHES, r=BLOCK)
+            out = z[:, part * BANK : (part + 1) * BANK].rearrange("p (s t b) -> p t s b", s=PARTS, b=BLOCK)
+            y = banks_of[unit][half][:].rearrange("p (t s b) -> p t s b", s=PARTS, b=BLOCK)
             scale_col = scale[:, half : half + 1]
             shift_col = shift[:, half : half + 1]
             if on_vector:
@@ -236,21 +323,24 @@ def tile_attention_pa_t_kernel(tc, x, qkv_w, qkv_g, qkv_b, out_q, out_k, out_v):
             else:
                 nc.scalar.activation(out=out, in_=y, func=ACT.Identity, bias=shift_col, scale=scale_col)
 
-        def store(out, stage, group, first=0, batches=GROUP_BATCHES):
-            batch = group * GROUP_BATCHES + first
-            nc.sync.dma_start(
-                out=out[batch : batch + batches].rearrange("b h (r t) j -> (h r) b (t j)", t=RUN_TOKENS),
-                in_=stage.rearrange("p (b c) -> p b c", b=batches),
-            )
+        def store(out, stage, first_unit, units):
+            for c in range(UNIT_BATCHES):
+                first = first_unit * UNIT_BATCHES + c
+                nc.sync.dma_start(
+                    out=out[first : first + (units - 1) * UNIT_BATCHES + 1 : UNIT_BATCHES].rearrange(
+                        "n h (r t) j -> (h r) n (t j)", t=RUN_TOKENS
+                    ),
+                    in_=stage[c:P:UNIT_BATCHES].rearrange("p (n m) -> p n m", n=units),
+                )
 
         def finish_v(z, group, pieces):
             stage = stage_pool.tile([P, GROUP_COLS], F32, align_bytes=64, name="stage_v")
             width = GROUP_COLS // pieces
-            batches = GROUP_BATCHES // pieces
+            units = GROUP_UNITS // pieces
             for piece in range(pieces):
                 cols = slice(piece * width, (piece + 1) * width)
                 nc.vector.transpose(stage[:, cols], z[:, cols])
-                store(out_v, stage[:, cols], group, piece * batches, batches)
+                store(out_v, stage[:, cols], group * GROUP_UNITS + piece * units, units)
 
         def finish_qk(z, group):
             turned = z_pool.tile([P, GROUP_COLS], F32, align_bytes=64, name="turned")
@@ -264,8 +354,8 @@ def tile_attention_pa_t_kernel(tc, x, qkv_w, qkv_g, qkv_b, out_q, out_k, out_v):
                 op0=ALU.mult,
                 op1=ALU.add,
             )
-            store(out_q, stage[:, 0], group)
-            store(out_k, stage[:, 1], group)
+            store(out_q, stage[:, 0], group * GROUP_UNITS, GROUP_UNITS)
+            store(out_k, stage[:, 1], group * GROUP_UNITS, GROUP_UNITS)
 
         for step, group in enumerate(order):
             first, second = range(group * GROUP_UNITS, (group + 1) * GROUP_UNITS)
@@ -286,4 +376,4 @@ def tile_attention_pa_t_kernel(tc, x, qkv_w, qkv_g, qkv_b, out_q, out_k, out_v):
                 normalise(z_v, second, V)
                 finish_v(z_v, group, 2 if step == GROUPS - 1 else 1)
             if step + 2 < GROUPS:
-                multiply_group(order[step + 2])
+                multiply_group(step + 2)

@@ -30,16 +30,15 @@ BLOCK = 32
 UNIT_TOKENS = BANK // P
 TOKENS_PER_BANK = BANK // WORDS
 UNIT_BATCHES = BANK // TOKENS
-RUNS = BLOCK // UNIT_BATCHES
-RUN_TOKENS = TOKENS // RUNS
-PARTS = RUN_TOKENS // UNIT_TOKENS
+RUN_TOKENS = TOKENS // BLOCK
+PARTS = P // BLOCK
 GROUP_UNITS = 2
 GROUP_BATCHES = GROUP_UNITS * UNIT_BATCHES
 GROUP_COLS = GROUP_UNITS * BANK
 UNITS = ROWS // BANK
 GROUPS = UNITS // GROUP_UNITS
 BN_STATS_DIM = 6
-SCALAR_UNITS = range(1, 13, 3)
+SCALAR_UNITS = range(1, 14, 3)
 LAG = 2
 
 FLOPS = 2 * ROWS * CHANNELS * FEATURES
@@ -92,8 +91,8 @@ def tile_attention_pa_t_kernel(tc, x, qkv_w, qkv_g, qkv_b, out_q, out_k, out_v):
         make_identity(nc, identity[:])
         row_order = const.tile([P, P], F32)
         nc.vector.tensor_copy(
-            out=row_order[:].rearrange("p (s r c) -> p s r c", r=RUNS, c=UNIT_BATCHES),
-            in_=identity[:].rearrange("p (c r s) -> p s r c", r=RUNS, c=UNIT_BATCHES),
+            out=row_order[:].rearrange("p (c s r) -> p c s r", c=UNIT_BATCHES, r=BLOCK),
+            in_=identity[:].rearrange("p (c r s) -> p c s r", c=UNIT_BATCHES, r=BLOCK),
         )
 
         w_codes = const.tile([P, FEATURES], U32, align_bytes=64)
@@ -255,9 +254,7 @@ def tile_attention_pa_t_kernel(tc, x, qkv_w, qkv_g, qkv_b, out_q, out_k, out_v):
                 transpose_x(step)
             if 1 <= step <= UNITS:
                 quantise_x(step - 1)
-            if step == 1:
-                measure(0)
-            if step > LAG:
+            if step >= LAG:
                 measure(step - LAG)
             if step - LAG in SCALAR_UNITS:
                 measure_on_scalar(step - LAG, ACT.Identity, sums)
@@ -265,15 +262,15 @@ def tile_attention_pa_t_kernel(tc, x, qkv_w, qkv_g, qkv_b, out_q, out_k, out_v):
                 measure_on_scalar(step - LAG - 1, ACT.Square, squares)
             if step - LAG - 1 == SCALAR_UNITS[-1]:
                 joined = join_scalar_units()
-            if step == UNITS:
-                nc.vector.tensor_copy(
-                    out=stats[:, QK, SCALAR_UNITS.start : SCALAR_UNITS.stop : SCALAR_UNITS.step, :],
-                    in_=joined[:],
-                )
             if step == UNITS // 2:
                 sort_gain_shift()
             if step == UNITS // 2 + 1:
                 turn_gain_shift()
+
+        nc.vector.tensor_copy(
+            out=stats[:, QK, SCALAR_UNITS.start : SCALAR_UNITS.stop : SCALAR_UNITS.step, :],
+            in_=joined[:],
+        )
 
         order = [GROUPS - 1] + list(range(GROUPS - 1))
 
@@ -312,8 +309,8 @@ def tile_attention_pa_t_kernel(tc, x, qkv_w, qkv_g, qkv_b, out_q, out_k, out_v):
 
         def normalise(z, unit, half, on_vector=False):
             part = unit % GROUP_UNITS
-            out = z[:, part * BANK : (part + 1) * BANK].rearrange("p (s t b) -> p t s b", s=PARTS, b=BLOCK)
-            y = banks_of[unit][half][:].rearrange("p (t s b) -> p t s b", s=PARTS, b=BLOCK)
+            out = z[:, part * BANK : (part + 1) * BANK].rearrange("p (a t r) -> p t a r", a=PARTS, r=BLOCK)
+            y = banks_of[unit][half][:].rearrange("p (t a r) -> p t a r", a=PARTS, r=BLOCK)
             scale_col = scale[:, half : half + 1]
             shift_col = shift[:, half : half + 1]
             if on_vector:
@@ -324,14 +321,11 @@ def tile_attention_pa_t_kernel(tc, x, qkv_w, qkv_g, qkv_b, out_q, out_k, out_v):
                 nc.scalar.activation(out=out, in_=y, func=ACT.Identity, bias=shift_col, scale=scale_col)
 
         def store(out, stage, first_unit, units):
-            for c in range(UNIT_BATCHES):
-                first = first_unit * UNIT_BATCHES + c
-                nc.sync.dma_start(
-                    out=out[first : first + (units - 1) * UNIT_BATCHES + 1 : UNIT_BATCHES].rearrange(
-                        "n h (r t) j -> (h r) n (t j)", t=RUN_TOKENS
-                    ),
-                    in_=stage[c:P:UNIT_BATCHES].rearrange("p (n m) -> p n m", n=units),
-                )
+            first, batches = first_unit * UNIT_BATCHES, units * UNIT_BATCHES
+            nc.sync.dma_start(
+                out=out[first : first + batches].rearrange("b h (r t) j -> (h r) b (t j)", t=RUN_TOKENS),
+                in_=stage.rearrange("p (b m) -> p b m", b=batches),
+            )
 
         def finish_v(z, group, pieces):
             stage = stage_pool.tile([P, GROUP_COLS], F32, align_bytes=64, name="stage_v")
@@ -342,20 +336,22 @@ def tile_attention_pa_t_kernel(tc, x, qkv_w, qkv_g, qkv_b, out_q, out_k, out_v):
                 nc.vector.transpose(stage[:, cols], z[:, cols])
                 store(out_v, stage[:, cols], group * GROUP_UNITS + piece * units, units)
 
-        def finish_qk(z, group):
+        def finish_qk(z, group, pieces):
             turned = z_pool.tile([P, GROUP_COLS], F32, align_bytes=64, name="turned")
-            nc.vector.transpose(turned[:], z[:])
             stage = stage_pool.tile([P, 2, GROUP_COLS // 2], F32, name="stage_qk")
-            nc.gpsimd.tensor_scalar(
-                out=stage[:].rearrange("p e (c j) -> p c e j", j=QK_DIM),
-                in0=turned[:].rearrange("p (c e j) -> p c e j", e=2, j=QK_DIM),
-                scalar1=1.0,
-                scalar2=0.0,
-                op0=ALU.mult,
-                op1=ALU.add,
-            )
-            store(out_q, stage[:, 0], group * GROUP_UNITS, GROUP_UNITS)
-            store(out_k, stage[:, 1], group * GROUP_UNITS, GROUP_UNITS)
+            width = GROUP_COLS // pieces
+            units = GROUP_UNITS // pieces
+            for piece in range(pieces):
+                cols = slice(piece * width, (piece + 1) * width)
+                part_cols = slice(piece * width // 2, (piece + 1) * width // 2)
+                nc.vector.transpose(turned[:, cols], z[:, cols])
+                parted = stage[:, :, part_cols].rearrange("p e (c j) -> p c e j", j=QK_DIM)
+                mixed = turned[:, cols].rearrange("p (c e j) -> p c e j", e=2, j=QK_DIM)
+                nc.gpsimd.tensor_scalar(
+                    out=parted, in0=mixed, scalar1=1.0, scalar2=0.0, op0=ALU.mult, op1=ALU.add
+                )
+                for part, out in enumerate((out_q, out_k)):
+                    store(out, stage[:, part, part_cols], group * GROUP_UNITS + piece * units, units)
 
         for step, group in enumerate(order):
             first, second = range(group * GROUP_UNITS, (group + 1) * GROUP_UNITS)
@@ -363,17 +359,18 @@ def tile_attention_pa_t_kernel(tc, x, qkv_w, qkv_g, qkv_b, out_q, out_k, out_v):
             z_v = z_pool.tile([P, GROUP_COLS], F32, align_bytes=64, name="z_v")
             if step == 0:
                 normalise(z_v, first, V)
-                normalise(z_v, second, V, on_vector=True)
+                normalise(z_v, second, V)
                 finish_v(z_v, group, 2)
                 normalise(z_qk, first, QK)
-                normalise(z_qk, second, QK)
-                finish_qk(z_qk, group)
+                normalise(z_qk, second, QK, on_vector=True)
+                finish_qk(z_qk, group, 2)
             else:
+                pieces = 2 if step == GROUPS - 1 else 1
                 normalise(z_qk, first, QK)
                 normalise(z_qk, second, QK)
-                finish_qk(z_qk, group)
+                finish_qk(z_qk, group, pieces)
                 normalise(z_v, first, V)
                 normalise(z_v, second, V)
-                finish_v(z_v, group, 2 if step == GROUPS - 1 else 1)
+                finish_v(z_v, group, pieces)
             if step + 2 < GROUPS:
                 multiply_group(step + 2)

@@ -38,7 +38,7 @@ GROUP_COLS = GROUP_UNITS * BANK
 UNITS = ROWS // BANK
 GROUPS = UNITS // GROUP_UNITS
 BN_STATS_DIM = 6
-SCALAR_UNITS = range(1, 14, 3)
+SCALAR_UNITS = range(1, 13, 3)
 LAG = 2
 
 FLOPS = 2 * ROWS * CHANNELS * FEATURES
@@ -262,15 +262,15 @@ def tile_attention_pa_t_kernel(tc, x, qkv_w, qkv_g, qkv_b, out_q, out_k, out_v):
                 measure_on_scalar(step - LAG - 1, ACT.Square, squares)
             if step - LAG - 1 == SCALAR_UNITS[-1]:
                 joined = join_scalar_units()
+            if step == UNITS:
+                nc.vector.tensor_copy(
+                    out=stats[:, QK, SCALAR_UNITS.start : SCALAR_UNITS.stop : SCALAR_UNITS.step, :],
+                    in_=joined[:],
+                )
             if step == UNITS // 2:
                 sort_gain_shift()
             if step == UNITS // 2 + 1:
                 turn_gain_shift()
-
-        nc.vector.tensor_copy(
-            out=stats[:, QK, SCALAR_UNITS.start : SCALAR_UNITS.stop : SCALAR_UNITS.step, :],
-            in_=joined[:],
-        )
 
         order = [GROUPS - 1] + list(range(GROUPS - 1))
 

from contextlib import ExitStack

import concourse.mybir as mybir
from concourse.masks import make_identity

F32 = mybir.dt.float32
BF16 = mybir.dt.bfloat16
U32 = mybir.dt.uint32
U8 = mybir.dt.uint8
FP8X4 = mybir.dt.float8_e4m3fn_x4
ACT = mybir.ActivationFunctionType
ALU = mybir.AluOpType

P = 128
BATCHES, TOKENS, CHANNELS = 32, 256, 512
HEADS, QK_DIM, V_DIM = 4, 16, 32
HEAD_FEATURES = 2 * QK_DIM + V_DIM
FEATURES = HEADS * HEAD_FEATURES
HALVES = FEATURES // P
QK, V = 0, 1
ROWS = BATCHES * TOKENS
EPS = 1e-5

PACK = 4
WORDS = CHANNELS // 2
WORD_PLANES = WORDS // P

BANK = 512
BLOCK = 32
UNIT_TOKENS = BANK // P
TOKENS_PER_BANK = BANK // WORDS
UNIT_BATCHES = BANK // TOKENS
RUN_TOKENS = TOKENS // BLOCK
PARTS = P // BLOCK
GROUP_UNITS = 2
GROUP_BATCHES = GROUP_UNITS * UNIT_BATCHES
GROUP_COLS = GROUP_UNITS * BANK
UNITS = ROWS // BANK
GROUPS = UNITS // GROUP_UNITS
BN_STATS_DIM = 6
SCALAR_UNITS = range(1, 13, 3)
LAG = 2

FLOPS = 2 * ROWS * CHANNELS * FEATURES


def tile_attention_pa_t_kernel(tc, x, qkv_w, qkv_g, qkv_b, out_q, out_k, out_v):
    nc = tc.nc
    with ExitStack() as ctx:
        const = ctx.enter_context(tc.tile_pool(name="const", bufs=1))
        x_pool = ctx.enter_context(tc.tile_pool(name="x_rows", bufs=UNITS))
        grouped_pool = ctx.enter_context(tc.tile_pool(name="grouped", bufs=3))
        unused_pool = ctx.enter_context(tc.tile_pool(name="unused", bufs=2))
        z_pool = ctx.enter_context(tc.tile_pool(name="z", bufs=2))
        stage_pool = ctx.enter_context(tc.tile_pool(name="stage", bufs=4))
        psum_t = ctx.enter_context(tc.psum_pool(name="psum_t", bufs=4))
        psum_y = ctx.enter_context(tc.psum_pool(name="psum_y", bufs=4))
        ctx.enter_context(tc.manual_schedule())

        w_rows = const.tile([P, HALVES * CHANNELS], BF16)
        gb_rows = const.tile([P, FEATURES], BF16)
        nc.gpsimd.memset(gb_rows[:], 0.0)
        x_units = x.flatten_outer_dims().rearrange("(n p t) k -> n p (t k)", p=P, t=UNIT_TOKENS)
        x_rows = []
        for unit in range(UNITS):
            x_tile = x_pool.tile([P, UNIT_TOKENS * CHANNELS], BF16, name="x_tile")
            source = x_units[unit]
            pieces = UNIT_TOKENS // TOKENS_PER_BANK if unit == 0 else 1
            width = UNIT_TOKENS * CHANNELS // pieces
            for piece in range(pieces):
                cols = slice(piece * width, (piece + 1) * width)
                nc.sync.dma_start(out=x_tile[:, cols], in_=source[:, cols])
                if unit == 0 and piece == 0:
                    nc.sync.dma_start(
                        out=w_rows[:].rearrange("p (s k) -> p s k", s=HALVES),
                        in_=qkv_w.rearrange("(s p) k -> p s k", s=HALVES),
                    )
            x_rows.append(x_tile)
            if unit == 3:
                nc.sync.dma_start(out=gb_rows[0:1, :], in_=qkv_g.rearrange("(o f) -> o f", o=1))
                nc.sync.dma_start(out=gb_rows[1:2, :], in_=qkv_b.rearrange("(o f) -> o f", o=1))

        one = const.tile([P, 1], F32)
        nc.vector.memset(one[:], 1.0)
        table_warm = const.tile([P, 1], F32)
        nc.scalar.activation(out=table_warm[:], in_=one[:], func=ACT.Abs_reciprocal_sqrt)
        eps = const.tile([P, 1], F32)
        nc.vector.memset(eps[:], 0.0)
        nc.vector.tensor_scalar(out=eps[:], in0=eps[:], scalar1=EPS, scalar2=None, op0=ALU.add)
        identity = const.tile([P, P], F32)
        make_identity(nc, identity[:])
        row_order = const.tile([P, P], F32)
        nc.vector.tensor_copy(
            out=row_order[:].rearrange("p (c s r) -> p c s r", c=UNIT_BATCHES, r=BLOCK),
            in_=identity[:].rearrange("p (c r s) -> p c s r", c=UNIT_BATCHES, r=BLOCK),
        )

        w_codes = const.tile([P, FEATURES], U32, align_bytes=64)
        w_scales = const.tile([P, FEATURES], U8, align_bytes=64)

        def prepare_weights():
            w_words = w_rows[:].bitcast(F32)
            wt = psum_t.tile([P, HALVES, WORD_PLANES, P], F32, tag="bank")
            for s in range(HALVES):
                for u in range(WORD_PLANES):
                    words_u = slice(s * WORDS + u, (s + 1) * WORDS, WORD_PLANES)
                    nc.tensor.transpose(wt[:, s, u, :], w_words[:, words_u], identity[:])
            w_grouped = const.tile([P, FEATURES * PACK], BF16, align_bytes=64)
            w_by_half = w_grouped[:].bitcast(F32).rearrange(
                "p (half h j u) -> p half h j u", half=HALVES, h=HEADS, u=WORD_PLANES
            )
            heads_here = HEADS // HALVES
            for s in range(HALVES):
                by_head = wt[:, s].rearrange("p u (h half j) -> p half h j u", h=heads_here, half=HALVES)
                for half in range(HALVES):
                    nc.vector.tensor_copy(
                        out=w_by_half[:, half, s * heads_here : (s + 1) * heads_here],
                        in_=by_head[:, half],
                    )
            nc.vector.quantize_mx(
                out=w_codes[:].bitcast(FP8X4), scales=w_scales[:], in_=w_grouped[:]
            )

        gb_sorted = const.tile([P, FEATURES], F32)
        gain_shift = const.tile([P, HALVES, 2], F32)
        minus_gain = const.tile([P, HALVES], F32)

        def sort_gain_shift():
            for half in range(HALVES):
                nc.vector.tensor_copy(
                    out=gb_sorted[:, half * P : (half + 1) * P].rearrange("p (h j) -> p h j", h=HEADS),
                    in_=gb_rows[:].rearrange("p (h half j) -> p half h j", h=HEADS, half=HALVES)[:, half],
                )

        def turn_gain_shift():
            gb_t = psum_t.tile([P, HALVES, P], F32, tag="bank")
            for half in range(HALVES):
                nc.tensor.transpose(
                    gb_t[:, half, :], gb_sorted[:, half * P : (half + 1) * P], identity[:]
                )
            nc.vector.tensor_copy(out=gain_shift[:], in_=gb_t[:, :, 0:2])
            nc.gpsimd.tensor_scalar(
                out=minus_gain[:], in0=gain_shift[:, :, 0], scalar1=-1.0, scalar2=None, op0=ALU.mult
            )

        x_codes = const.tile([P, ROWS], U32, align_bytes=64)
        x_scales = const.tile([P, ROWS], U8, align_bytes=64)

        def multiply(unit, psum):
            cols = slice(unit * BANK, (unit + 1) * BANK)
            banks = []
            for half in range(HALVES):
                features = slice(half * P, (half + 1) * P)
                y = psum.tile([P, BANK], F32, tag="bank")
                nc.tensor.matmul_mx(
                    out=y[:],
                    lhsT=w_codes[:, features].bitcast(FP8X4),
                    lhsT_scale=w_scales[:, features],
                    rhs=x_codes[:, cols].bitcast(FP8X4),
                    rhs_scale=x_scales[:, cols],
                    start=True,
                    stop=True,
                )
                banks.append(y)
            return banks

        stats = const.tile([P, HALVES, UNITS, BN_STATS_DIM], F32)
        minus_center = const.tile([P, 1], F32)
        sums = const.tile([P, len(SCALAR_UNITS)], F32)
        squares = const.tile([P, len(SCALAR_UNITS)], F32)
        grouped_of = {}
        banks_of = {}

        def transpose_x(unit):
            words = x_rows[unit][:].bitcast(F32)
            grouped = grouped_pool.tile([P, BANK * PACK], BF16, align_bytes=64)
            grouped_words = grouped[:].bitcast(F32).rearrange(
                "p (t c u) -> p t c u", t=UNIT_TOKENS, u=WORD_PLANES
            )
            for first_token in range(0, UNIT_TOKENS, TOKENS_PER_BANK):
                xt = psum_t.tile([P, TOKENS_PER_BANK, WORD_PLANES, P], F32, tag="bank")
                for t in range(TOKENS_PER_BANK):
                    for u in range(WORD_PLANES):
                        token = first_token + t
                        words_u = slice(token * WORDS + u, (token + 1) * WORDS, WORD_PLANES)
                        nc.tensor.transpose(xt[:, t, u, :], words[:, words_u], row_order[:])
                nc.scalar.copy(
                    out=grouped_words[:, first_token : first_token + TOKENS_PER_BANK],
                    in_=xt[:].rearrange("p t u c -> p t c u"),
                )
                if unit == 0 and first_token == 0:
                    prepare_weights()
            grouped_of[unit] = grouped

        def quantise_x(unit):
            cols = slice(unit * BANK, (unit + 1) * BANK)
            nc.vector.quantize_mx(
                out=x_codes[:, cols].bitcast(FP8X4),
                scales=x_scales[:, cols],
                in_=grouped_of[unit][:],
            )

        def measure(unit):
            banks_of[unit] = multiply(unit, psum_y)
            for half, y in enumerate(banks_of[unit]):
                if not (half == QK and unit in SCALAR_UNITS):
                    nc.vector.bn_stats(out=stats[:, half, unit, :], in_=y[:])
            if unit == 0:
                nc.gpsimd.tensor_scalar(
                    out=minus_center[:], in0=stats[:, QK, 0, 1:2], scalar1=-1.0, scalar2=None, op0=ALU.mult
                )

        def measure_on_scalar(unit, func, total):
            i = SCALAR_UNITS.index(unit)
            unused = unused_pool.tile([P, BANK], BF16)
            nc.scalar.activation(
                out=unused[:],
                in_=banks_of[unit][QK][:],
                func=func,
                bias=minus_center[:],
                accum_out=total[:, i : i + 1],
            )

        def join_scalar_units():
            count = len(SCALAR_UNITS)
            offset = const.tile([P, count], F32)
            nc.gpsimd.tensor_scalar(
                out=offset[:], in0=sums[:], scalar1=1.0 / BANK, scalar2=None, op0=ALU.mult
            )
            spread = const.tile([P, count], F32)
            nc.gpsimd.tensor_tensor(out=spread[:], in0=offset[:], in1=sums[:], op=ALU.mult)
            nc.gpsimd.tensor_tensor(out=spread[:], in0=squares[:], in1=spread[:], op=ALU.subtract)
            joined = const.tile([P, count, BN_STATS_DIM], F32)
            nc.gpsimd.memset(joined[:], BANK / 2)
            for part in range(2):
                nc.gpsimd.tensor_scalar(
                    out=joined[:, :, 3 * part + 1],
                    in0=offset[:],
                    scalar1=minus_center[:],
                    scalar2=None,
                    op0=ALU.subtract,
                )
                nc.gpsimd.tensor_scalar(
                    out=joined[:, :, 3 * part + 2],
                    in0=spread[:],
                    scalar1=0.5,
                    scalar2=None,
                    op0=ALU.mult,
                )
            return joined

        for step in range(UNITS + LAG):
            if step < UNITS:
                transpose_x(step)
            if 1 <= step <= UNITS:
                quantise_x(step - 1)
            if step >= LAG:
                measure(step - LAG)
            if step - LAG in SCALAR_UNITS:
                measure_on_scalar(step - LAG, ACT.Identity, sums)
            if step - LAG - 1 in SCALAR_UNITS:
                measure_on_scalar(step - LAG - 1, ACT.Square, squares)
            if step - LAG - 1 == SCALAR_UNITS[-1]:
                joined = join_scalar_units()
            if step == UNITS:
                nc.vector.tensor_copy(
                    out=stats[:, QK, SCALAR_UNITS.start : SCALAR_UNITS.stop : SCALAR_UNITS.step, :],
                    in_=joined[:],
                )
            if step == UNITS // 2:
                sort_gain_shift()
            if step == UNITS // 2 + 1:
                turn_gain_shift()

        order = [GROUPS - 1] + list(range(GROUPS - 1))

        def multiply_group(step):
            group = order[step]
            for unit in range(group * GROUP_UNITS, (group + 1) * GROUP_UNITS):
                banks_of[unit] = multiply(unit, psum_t if step % 2 else psum_y)

        multiply_group(1)

        mean_var = const.tile([P, HALVES, 2], F32)
        for half in range(HALVES):
            nc.vector.bn_aggr(
                out=mean_var[:, half, :], in_=stats[:, half].rearrange("p u s -> p (u s)")
            )
        inv_std = const.tile([P, HALVES], F32)
        nc.scalar.activation(
            out=inv_std[:], in_=mean_var[:, :, 1], func=ACT.Abs_reciprocal_sqrt, bias=eps[:]
        )
        mean_gain = const.tile([P, HALVES], F32)
        nc.vector.tensor_tensor(
            out=mean_gain[:], in0=mean_var[:, :, 0], in1=minus_gain[:], op=ALU.mult
        )
        scale = const.tile([P, HALVES], F32)
        nc.vector.tensor_tensor(out=scale[:], in0=gain_shift[:, :, 0], in1=inv_std[:], op=ALU.mult)
        shift = const.tile([P, HALVES], F32)
        for half in (V, QK):
            nc.vector.scalar_tensor_tensor(
                out=shift[:, half : half + 1],
                in0=mean_gain[:, half : half + 1],
                scalar=inv_std[:, half : half + 1],
                in1=gain_shift[:, half, 1:2],
                op0=ALU.mult,
                op1=ALU.add,
            )

        def normalise(z, unit, half, on_vector=False):
            part = unit % GROUP_UNITS
            out = z[:, part * BANK : (part + 1) * BANK].rearrange("p (a t r) -> p t a r", a=PARTS, r=BLOCK)
            y = banks_of[unit][half][:].rearrange("p (t a r) -> p t a r", a=PARTS, r=BLOCK)
            scale_col = scale[:, half : half + 1]
            shift_col = shift[:, half : half + 1]
            if on_vector:
                nc.vector.tensor_scalar(
                    out=out, in0=y, scalar1=scale_col, scalar2=shift_col, op0=ALU.mult, op1=ALU.add
                )
            else:
                nc.scalar.activation(out=out, in_=y, func=ACT.Identity, bias=shift_col, scale=scale_col)

        def store(out, stage, first_unit, units):
            first, batches = first_unit * UNIT_BATCHES, units * UNIT_BATCHES
            nc.sync.dma_start(
                out=out[first : first + batches].rearrange("b h (r t) j -> (h r) b (t j)", t=RUN_TOKENS),
                in_=stage.rearrange("p (b m) -> p b m", b=batches),
            )

        def finish_v(z, group, pieces):
            stage = stage_pool.tile([P, GROUP_COLS], F32, align_bytes=64, name="stage_v")
            width = GROUP_COLS // pieces
            units = GROUP_UNITS // pieces
            for piece in range(pieces):
                cols = slice(piece * width, (piece + 1) * width)
                nc.vector.transpose(stage[:, cols], z[:, cols])
                store(out_v, stage[:, cols], group * GROUP_UNITS + piece * units, units)

        def finish_qk(z, group, pieces):
            turned = z_pool.tile([P, GROUP_COLS], F32, align_bytes=64, name="turned")
            stage = stage_pool.tile([P, 2, GROUP_COLS // 2], F32, name="stage_qk")
            width = GROUP_COLS // pieces
            units = GROUP_UNITS // pieces
            for piece in range(pieces):
                cols = slice(piece * width, (piece + 1) * width)
                part_cols = slice(piece * width // 2, (piece + 1) * width // 2)
                nc.vector.transpose(turned[:, cols], z[:, cols])
                parted = stage[:, :, part_cols].rearrange("p e (c j) -> p c e j", j=QK_DIM)
                mixed = turned[:, cols].rearrange("p (c e j) -> p c e j", e=2, j=QK_DIM)
                nc.gpsimd.tensor_scalar(
                    out=parted, in0=mixed, scalar1=1.0, scalar2=0.0, op0=ALU.mult, op1=ALU.add
                )
                for part, out in enumerate((out_q, out_k)):
                    store(out, stage[:, part, part_cols], group * GROUP_UNITS + piece * units, units)

        for step, group in enumerate(order):
            first, second = range(group * GROUP_UNITS, (group + 1) * GROUP_UNITS)
            z_qk = z_pool.tile([P, GROUP_COLS], F32, align_bytes=64, name="z_qk")
            z_v = z_pool.tile([P, GROUP_COLS], F32, align_bytes=64, name="z_v")
            if step == 0:
                normalise(z_v, first, V)
                normalise(z_v, second, V)
                finish_v(z_v, group, 2)
                normalise(z_qk, first, QK)
                normalise(z_qk, second, QK, on_vector=True)
                finish_qk(z_qk, group, 2)
            else:
                pieces = 2 if step == GROUPS - 1 else 1
                normalise(z_qk, first, QK)
                normalise(z_qk, second, QK)
                finish_qk(z_qk, group, pieces)
                normalise(z_v, first, V)
                normalise(z_v, second, V)
                finish_v(z_v, group, pieces)
            if step + 2 < GROUPS:
                multiply_group(step + 2)
